import numpy as np
import ml_dtypes


def mxq(x, axis, fmt="e4m3"):
    dtype, down = {"e4m3": (ml_dtypes.float8_e4m3fn, 7), "e5m2": (ml_dtypes.float8_e5m2, 14)}[fmt]
    v = np.moveaxis(np.asarray(x, np.float32).astype(ml_dtypes.bfloat16).astype(np.float64), axis, -1)
    blocks = v.reshape(v.shape[:-1] + (-1, 32))
    amax = np.abs(blocks).max(-1, keepdims=True)
    byte = np.maximum(np.where(amax > 0, np.frexp(amax)[1] - 1 + 127, 0) - down, 1)
    scale = np.exp2(byte - 127.0)
    codes = (blocks / scale).astype(np.float32).astype(dtype).astype(np.float64)
    return np.moveaxis((codes * scale).reshape(v.shape), -1, axis)


WIDE = False


def mx_kscale(k):
    if not WIDE:
        return np.ones(k)
    levels = np.array([20, -20, 10, -10, 0])
    a = np.random.permutation(np.resize(levels, k // 512 * 4)).reshape(k // 512, 4)
    idx = np.arange(k)
    return np.exp2(a[idx // 512, idx % 128 // 32])


BF16 = ml_dtypes.bfloat16


def bf(x):
    return np.asarray(x, np.float32).astype(BF16)


def f64(x):
    return np.asarray(x).astype(np.float64)


N, C, F, H, W, KH, KW = 512, 64, 128, 4, 4, 3, 3
P = H * W


def setup_inputs():
    s = mx_kscale(N)[:, None, None, None]
    x = np.random.standard_normal((N, C, H, W)) * 2.0 * s
    k = np.random.standard_normal((F, C, H, W)) * 2.0 / np.sqrt(C)
    g = np.random.standard_normal((N, F, H, W)) * np.exp2(np.random.randint(-12, 1, (N, 1, 1, 1))) / s
    return {"x_dct": bf(x), "k_dct": bf(k), "grad_out": bf(g)}


def reference(x_dct, k_dct, grad_out):
    xq = mxq(f64(x_dct), 0, "e4m3").reshape(N, C, P).transpose(2, 0, 1)
    gq = mxq(f64(grad_out), 0, "e5m2").reshape(N, F, P).transpose(2, 1, 0)
    r = gq @ xq
    return r.transpose(1, 2, 0).reshape(F, C, H, W)

@@ -1,0 +1,97 @@
+import concourse.mybir as mybir
+
+BF16 = mybir.dt.bfloat16
+F32 = mybir.dt.float32
+U32 = mybir.dt.uint32
+U8 = mybir.dt.uint8
+E4M3_X4 = mybir.dt.float8_e4m3fn_x4
+E5M2_X4 = mybir.dt.float8_e5m2_x4
+
+P = 128
+PACK = 4
+IMAGES = P * PACK
+CHANNELS = 64
+FILTERS = 128
+FREQS = 16
+RUN = 4
+GROUPS = FREQS // RUN
+N_MOVING = 512
+FREQS_MOVING = N_MOVING // CHANNELS
+G_CHUNKS = 2
+CHUNK_FILTERS = FILTERS // G_CHUNKS
+
+FLOPS = 2 * FREQS * FILTERS * CHANNELS * IMAGES
+BYTES = 2 * IMAGES * FREQS * (CHANNELS + FILTERS) + 4 * FILTERS * CHANNELS * FREQS
+
+
+def regroup(copy, raw, grouped, group):
+    src = raw.rearrange("p j (r a i) -> p a r j i", a=GROUPS, i=RUN)
+    dst = grouped.rearrange("p (a i) r j -> p a r j i", i=RUN)
+    copy(out=dst[:, group], in_=src[:, group])
+
+
+def tile_convdct_pa_s_kernel(tc, x_dct, k_dct, grad_out, out):
+    nc = tc.nc
+    copy_of_group = [nc.vector.tensor_copy] * (GROUPS // 2) + [nc.scalar.copy] * (GROUPS // 2)
+
+    x_rows = x_dct.rearrange("(p j) c h w -> p j (c h w)", j=PACK)
+    g_rows = grad_out.rearrange("(p j) f h w -> p j (f h w)", j=PACK)
+
+    with tc.tile_pool(name="keep", bufs=1) as keep, tc.psum_pool(name="psum", bufs=8) as psum:
+        x_raw = keep.tile([P, PACK, CHANNELS * FREQS], BF16)
+        nc.sync.dma_start(out=x_raw[:], in_=x_rows)
+        g_raw = []
+        for k in range(G_CHUNKS):
+            chunk = keep.tile([P, PACK, CHUNK_FILTERS * FREQS], BF16, name="g_raw%d" % k)
+            columns = slice(k * CHUNK_FILTERS * FREQS, (k + 1) * CHUNK_FILTERS * FREQS)
+            nc.sync.dma_start(out=chunk[:], in_=g_rows[:, :, columns])
+            g_raw.append(chunk)
+
+        x_grouped = keep.tile([P, FREQS, CHANNELS, PACK], BF16, align_bytes=64)
+        x_codes = keep.tile([P, FREQS // FREQS_MOVING, N_MOVING], U32, align_bytes=64)
+        x_scales = keep.tile([P, FREQS // FREQS_MOVING, N_MOVING], U8, align_bytes=64)
+        for group in range(GROUPS):
+            regroup(copy_of_group[group], x_raw[:], x_grouped[:], group)
+        for m in range(FREQS // FREQS_MOVING):
+            nc.vector.quantize_mx(
+                out=x_codes[:, m, :].bitcast(E4M3_X4),
+                scales=x_scales[:, m, :],
+                in_=x_grouped[:, m * FREQS_MOVING : (m + 1) * FREQS_MOVING].rearrange("p a c j -> p (a c j)"),
+            )
+
+        g_grouped = keep.tile([P, FREQS, FILTERS, PACK], BF16, align_bytes=64)
+        g_codes = keep.tile([P, FREQS, FILTERS], U32, align_bytes=64)
+        g_scales = keep.tile([P, FREQS, FILTERS], U8, align_bytes=64)
+        for k in range(G_CHUNKS):
+            filters = slice(k * CHUNK_FILTERS, (k + 1) * CHUNK_FILTERS)
+            for group in range(GROUPS):
+                regroup(copy_of_group[group], g_raw[k][:], g_grouped[:, :, filters, :], group)
+                if k == G_CHUNKS - 1:
+                    for freq in range(group * RUN, (group + 1) * RUN):
+                        nc.vector.quantize_mx(
+                            out=g_codes[:, freq, :].bitcast(E5M2_X4),
+                            scales=g_scales[:, freq, :],
+                            in_=g_grouped[:, freq].rearrange("p f j -> p (f j)"),
+                        )
+
+        planes = keep.tile([P, FREQS, CHANNELS], F32)
+        result = keep.tile([P, CHANNELS, FREQS], F32)
+        for group in range(GROUPS):
+            freqs = slice(group * RUN, (group + 1) * RUN)
+            for freq in range(group * RUN, (group + 1) * RUN):
+                m = freq // FREQS_MOVING
+                own = freq % FREQS_MOVING
+                acc = psum.tile([FILTERS, N_MOVING], F32)
+                nc.tensor.matmul_mx(
+                    out=acc[:],
+                    lhsT=g_codes[:, freq, :].bitcast(E5M2_X4),
+                    lhsT_scale=g_scales[:, freq, :],
+                    rhs=x_codes[:, m, :].bitcast(E4M3_X4),
+                    rhs_scale=x_scales[:, m, :],
+                    start=True,
+                    stop=True,
+                )
+                nc.scalar.copy(out=planes[:, freq, :], in_=acc[:, own * CHANNELS : (own + 1) * CHANNELS])
+            nc.vector.tensor_copy(out=result[:, :, freqs], in_=planes[:, freqs, :].rearrange("p i c -> p c i"))
+
+        nc.sync.dma_start(out=out.rearrange("f c h w -> f (c h w)"), in_=result[:].rearrange("p c a -> p (c a)"))

@@ -37,7 +37,7 @@ def tile_convdct_pa_s_kernel(tc, x_dct, k_dct, grad_out, out):
     x_rows = x_dct.rearrange("(p j) c h w -> p j (c h w)", j=PACK)
     g_rows = grad_out.rearrange("(p j) f h w -> p j (f h w)", j=PACK)
 
-    with tc.tile_pool(name="keep", bufs=1) as keep, tc.psum_pool(name="psum", bufs=8) as psum:
+    with tc.tile_pool(name="keep", bufs=1) as keep, tc.psum_pool(name="psum", bufs=8) as psum, tc.manual_schedule():
         x_raw = keep.tile([P, PACK, CHANNELS * FREQS], BF16)
         nc.sync.dma_start(out=x_raw[:], in_=x_rows)
         g_raw = []

@@ -4,6 +4,7 @@ BF16 = mybir.dt.bfloat16
 F32 = mybir.dt.float32
 U32 = mybir.dt.uint32
 U8 = mybir.dt.uint8
+I32 = mybir.dt.int32
 E4M3_X4 = mybir.dt.float8_e4m3fn_x4
 E5M2_X4 = mybir.dt.float8_e5m2_x4
 
@@ -18,6 +19,7 @@ GROUPS = FREQS // RUN
 N_MOVING = 512
 FREQS_MOVING = N_MOVING // CHANNELS
 G_CHUNKS = 2
+WARM_PASSES = 8
 CHUNK_FILTERS = FILTERS // G_CHUNKS
 
 FLOPS = 2 * FREQS * FILTERS * CHANNELS * IMAGES
@@ -32,7 +34,7 @@ def regroup(copy, raw, grouped, group):
 
 def tile_convdct_pa_s_kernel(tc, x_dct, k_dct, grad_out, out):
     nc = tc.nc
-    copy_of_group = [nc.vector.tensor_copy] * (GROUPS // 2) + [nc.scalar.copy] * (GROUPS // 2)
+    copy_of_group = [nc.vector.tensor_copy, nc.scalar.copy] * (GROUPS // 2)
 
     x_rows = x_dct.rearrange("(p j) c h w -> p j (c h w)", j=PACK)
     g_rows = grad_out.rearrange("(p j) f h w -> p j (f h w)", j=PACK)
@@ -47,6 +49,12 @@ def tile_convdct_pa_s_kernel(tc, x_dct, k_dct, grad_out, out):
             nc.sync.dma_start(out=chunk[:], in_=g_rows[:, :, columns])
             g_raw.append(chunk)
 
+        zeros = keep.tile([P, FILTERS * PACK], BF16, align_bytes=64)
+        zero_codes = keep.tile([P, FILTERS], U32, align_bytes=64)
+        zero_scales = keep.tile([P, FILTERS], U8, align_bytes=64)
+        nc.vector.memset(zeros[:].bitcast(I32), 0)
+        nc.vector.quantize_mx(out=zero_codes[:].bitcast(E5M2_X4), scales=zero_scales[:], in_=zeros[:])
+
         x_grouped = keep.tile([P, FREQS, CHANNELS, PACK], BF16, align_bytes=64)
         x_codes = keep.tile([P, FREQS // FREQS_MOVING, N_MOVING], U32, align_bytes=64)
         x_scales = keep.tile([P, FREQS // FREQS_MOVING, N_MOVING], U8, align_bytes=64)
@@ -57,6 +65,18 @@ def tile_convdct_pa_s_kernel(tc, x_dct, k_dct, grad_out, out):
                 out=x_codes[:, m, :].bitcast(E4M3_X4),
                 scales=x_scales[:, m, :],
                 in_=x_grouped[:, m * FREQS_MOVING : (m + 1) * FREQS_MOVING].rearrange("p a c j -> p (a c j)"),
+            )
+
+        warm = psum.tile([FILTERS, N_MOVING], F32, tag="acc")
+        for i in range(WARM_PASSES):
+            nc.tensor.matmul_mx(
+                out=warm[:],
+                lhsT=zero_codes[:].bitcast(E5M2_X4),
+                lhsT_scale=zero_scales[:],
+                rhs=x_codes[:, 0, :].bitcast(E4M3_X4),
+                rhs_scale=x_scales[:, 0, :],
+                start=True,
+                stop=True,
             )
 
         g_grouped = keep.tile([P, FREQS, FILTERS, PACK], BF16, align_bytes=64)

@@ -17,101 +17,173 @@ FREQS = 16
 RUN = 4
 GROUPS = FREQS // RUN
 N_MOVING = 512
-FREQS_MOVING = N_MOVING // CHANNELS
-G_CHUNKS = 2
-WARM_PASSES = 8
-CHUNK_FILTERS = FILTERS // G_CHUNKS
+X_CHUNKS = (16, 16, 32)
+G_CHUNKS = (32, 32, 32, 32)
+TWINS = 2
+UNIT = TWINS * CHANNELS
+SEQ_UNITS = 11
+UNIT_PLACE = (0, 6, 9, 4)
+ZERO_RUNS = ((1, 3), (5, 1), (7, 2), (10, 1))
+WARM_FIRST = 5
+WARM_SECOND = 3
 
 FLOPS = 2 * FREQS * FILTERS * CHANNELS * IMAGES
 BYTES = 2 * IMAGES * FREQS * (CHANNELS + FILTERS) + 4 * FILTERS * CHANNELS * FREQS
 
 
-def regroup(copy, raw, grouped, group):
-    src = raw.rearrange("p j (r a i) -> p a r j i", a=GROUPS, i=RUN)
-    dst = grouped.rearrange("p (a i) r j -> p a r j i", i=RUN)
-    copy(out=dst[:, group], in_=src[:, group])
-
-
 def tile_convdct_pa_s_kernel(tc, x_dct, k_dct, grad_out, out):
     nc = tc.nc
-    copy_of_group = [nc.vector.tensor_copy, nc.scalar.copy] * (GROUPS // 2)
-
     x_rows = x_dct.rearrange("(p j) c h w -> p j (c h w)", j=PACK)
     g_rows = grad_out.rearrange("(p j) f h w -> p j (f h w)", j=PACK)
 
-    with tc.tile_pool(name="keep", bufs=1) as keep, tc.psum_pool(name="psum", bufs=8) as psum, tc.manual_schedule():
-        x_raw = keep.tile([P, PACK, CHANNELS * FREQS], BF16)
-        nc.sync.dma_start(out=x_raw[:], in_=x_rows)
+    with tc.tile_pool(name="keep", bufs=1) as keep, tc.psum_pool(name="psum", bufs=1) as psum, tc.manual_schedule():
+        x_raw = []
+        x_first = []
+        first = 0
+        for c, rows in enumerate(X_CHUNKS):
+            chunk = keep.tile([P, PACK, rows * FREQS], BF16, name="x_raw%d" % c)
+            nc.sync.dma_start(out=chunk[:], in_=x_rows[:, :, first * FREQS : (first + rows) * FREQS])
+            x_raw.append(chunk)
+            x_first.append(first)
+            first += rows
         g_raw = []
-        for k in range(G_CHUNKS):
-            chunk = keep.tile([P, PACK, CHUNK_FILTERS * FREQS], BF16, name="g_raw%d" % k)
-            columns = slice(k * CHUNK_FILTERS * FREQS, (k + 1) * CHUNK_FILTERS * FREQS)
-            nc.sync.dma_start(out=chunk[:], in_=g_rows[:, :, columns])
+        g_first = []
+        first = 0
+        for c, rows in enumerate(G_CHUNKS):
+            chunk = keep.tile([P, PACK, rows * FREQS], BF16, name="g_raw%d" % c)
+            nc.sync.dma_start(out=chunk[:], in_=g_rows[:, :, first * FREQS : (first + rows) * FREQS])
             g_raw.append(chunk)
+            g_first.append(first)
+            first += rows
 
+        half = SEQ_UNITS * UNIT
+        x_width = TWINS * half + CHANNELS
+        x_codes = keep.tile([P, x_width], U32, align_bytes=64)
+        x_scales = keep.tile([P, x_width], U8, align_bytes=64)
+        nc.gpsimd.memset(x_scales[:].bitcast(F32), 0.0)
+        nc.gpsimd.memset(x_codes[:, half:].bitcast(F32), 0.0)
+        for start, count in ZERO_RUNS:
+            nc.vector.memset(x_codes[:, start * UNIT : (start + count) * UNIT].bitcast(I32), 0)
         zeros = keep.tile([P, FILTERS * PACK], BF16, align_bytes=64)
         zero_codes = keep.tile([P, FILTERS], U32, align_bytes=64)
         zero_scales = keep.tile([P, FILTERS], U8, align_bytes=64)
         nc.vector.memset(zeros[:].bitcast(I32), 0)
         nc.vector.quantize_mx(out=zero_codes[:].bitcast(E5M2_X4), scales=zero_scales[:], in_=zeros[:])
 
-        x_grouped = keep.tile([P, FREQS, CHANNELS, PACK], BF16, align_bytes=64)
-        x_codes = keep.tile([P, FREQS // FREQS_MOVING, N_MOVING], U32, align_bytes=64)
-        x_scales = keep.tile([P, FREQS // FREQS_MOVING, N_MOVING], U8, align_bytes=64)
-        for group in range(GROUPS):
-            regroup(copy_of_group[group], x_raw[:], x_grouped[:], group)
-        for m in range(FREQS // FREQS_MOVING):
-            nc.vector.quantize_mx(
-                out=x_codes[:, m, :].bitcast(E4M3_X4),
-                scales=x_scales[:, m, :],
-                in_=x_grouped[:, m * FREQS_MOVING : (m + 1) * FREQS_MOVING].rearrange("p a c j -> p (a c j)"),
-            )
-
-        warm = psum.tile([FILTERS, N_MOVING], F32, tag="acc")
-        for i in range(WARM_PASSES):
-            nc.tensor.matmul_mx(
-                out=warm[:],
-                lhsT=zero_codes[:].bitcast(E5M2_X4),
-                lhsT_scale=zero_scales[:],
-                rhs=x_codes[:, 0, :].bitcast(E4M3_X4),
-                rhs_scale=x_scales[:, 0, :],
-                start=True,
-                stop=True,
-            )
-
+        x_grouped = keep.tile([P, TWINS, RUN, TWINS, CHANNELS, PACK], BF16, align_bytes=64)
         g_grouped = keep.tile([P, FREQS, FILTERS, PACK], BF16, align_bytes=64)
-        g_codes = keep.tile([P, FREQS, FILTERS], U32, align_bytes=64)
-        g_scales = keep.tile([P, FREQS, FILTERS], U8, align_bytes=64)
-        for k in range(G_CHUNKS):
-            filters = slice(k * CHUNK_FILTERS, (k + 1) * CHUNK_FILTERS)
-            for group in range(GROUPS):
-                regroup(copy_of_group[group], g_raw[k][:], g_grouped[:, :, filters, :], group)
-                if k == G_CHUNKS - 1:
-                    for freq in range(group * RUN, (group + 1) * RUN):
-                        nc.vector.quantize_mx(
-                            out=g_codes[:, freq, :].bitcast(E5M2_X4),
-                            scales=g_scales[:, freq, :],
-                            in_=g_grouped[:, freq].rearrange("p f j -> p (f j)"),
-                        )
-
-        planes = keep.tile([P, FREQS, CHANNELS], F32)
+        g_codes = keep.tile([P, FREQS * FILTERS], U32, align_bytes=64)
+        g_scales = keep.tile([P, FREQS * FILTERS], U8, align_bytes=64)
         result = keep.tile([P, CHANNELS, FREQS], F32)
-        for group in range(GROUPS):
-            freqs = slice(group * RUN, (group + 1) * RUN)
-            for freq in range(group * RUN, (group + 1) * RUN):
-                m = freq // FREQS_MOVING
-                own = freq % FREQS_MOVING
-                acc = psum.tile([FILTERS, N_MOVING], F32)
+        banks = {}
+
+        def copy_x(copy, c, m):
+            rows = slice(x_first[c], x_first[c] + X_CHUNKS[c])
+            src = x_raw[c][:].rearrange("p j (r m s t) -> p m s r j t", m=TWINS, s=TWINS, t=RUN)
+            dst = x_grouped[:, :, :, :, rows, :].rearrange("p m t s r j -> p m s r j t")
+            copy(out=dst[:, m], in_=src[:, m])
+
+        def copy_g(copy, c, first_group, count):
+            rows = slice(g_first[c], g_first[c] + G_CHUNKS[c])
+            src = g_raw[c][:].rearrange("p j (r a t) -> p a r j t", a=GROUPS, t=RUN)
+            dst = g_grouped[:, :, rows, :].rearrange("p (a t) r j -> p a r j t", t=RUN)
+            copy(out=dst[:, first_group : first_group + count], in_=src[:, first_group : first_group + count])
+
+        def quantise_x(m, t):
+            start = (m * SEQ_UNITS + UNIT_PLACE[t]) * UNIT
+            nc.vector.quantize_mx(
+                out=x_codes[:, start : start + UNIT].bitcast(E4M3_X4),
+                scales=x_scales[:, start : start + UNIT],
+                in_=x_grouped[:, m, t].rearrange("p s r j -> p (s r j)"),
+            )
+
+        def quantise_g(first_freq, count):
+            columns = slice(first_freq * FILTERS, (first_freq + count) * FILTERS)
+            nc.vector.quantize_mx(
+                out=g_codes[:, columns].bitcast(E5M2_X4),
+                scales=g_scales[:, columns],
+                in_=g_grouped[:, first_freq : first_freq + count].rearrange("p a f j -> p (a f j)"),
+            )
+
+        def window(group, t):
+            m = group // TWINS
+            s = group % TWINS
+            start = (m * SEQ_UNITS + UNIT_PLACE[t] - t) * UNIT + s * CHANNELS
+            return slice(start, start + N_MOVING)
+
+        warm = psum.tile([P, N_MOVING], F32, name="warm")
+
+        def warm_up(group, count):
+            for i in range(count):
                 nc.tensor.matmul_mx(
-                    out=acc[:],
-                    lhsT=g_codes[:, freq, :].bitcast(E5M2_X4),
-                    lhsT_scale=g_scales[:, freq, :],
-                    rhs=x_codes[:, m, :].bitcast(E4M3_X4),
-                    rhs_scale=x_scales[:, m, :],
+                    out=warm[:],
+                    lhsT=zero_codes[:].bitcast(E5M2_X4),
+                    lhsT_scale=zero_scales[:],
+                    rhs=x_codes[:, window(group, 0)].bitcast(E4M3_X4),
+                    rhs_scale=x_scales[:, window(group, 0)],
                     start=True,
                     stop=True,
                 )
-                nc.scalar.copy(out=planes[:, freq, :], in_=acc[:, own * CHANNELS : (own + 1) * CHANNELS])
-            nc.vector.tensor_copy(out=result[:, :, freqs], in_=planes[:, freqs, :].rearrange("p i c -> p c i"))
 
+        def passes(group):
+            bank = psum.tile([P, N_MOVING], F32, name="bank%d" % group)
+            banks[group] = bank
+            for t in range(RUN):
+                freq = group * RUN + t
+                columns = slice(freq * FILTERS, (freq + 1) * FILTERS)
+                nc.tensor.matmul_mx(
+                    out=bank[:],
+                    lhsT=g_codes[:, columns].bitcast(E5M2_X4),
+                    lhsT_scale=g_scales[:, columns],
+                    rhs=x_codes[:, window(group, t)].bitcast(E4M3_X4),
+                    rhs_scale=x_scales[:, window(group, t)],
+                    start=(t == 0),
+                    stop=(t == RUN - 1),
+                )
+
+        def empty(copy, group):
+            wanted = banks[group][:].rearrange("p (t e c) -> p e c t", t=RUN, e=TWINS)
+            copy(out=result[:, :, group * RUN : (group + 1) * RUN], in_=wanted[:, 0])
+
+        V = nc.vector.tensor_copy
+        S = nc.scalar.copy
+        copy_x(V, 0, 0)
+        copy_x(S, 0, 1)
+        copy_x(V, 1, 0)
+        copy_x(V, 1, 1)
+        copy_x(V, 2, 0)
+        copy_x(S, 2, 1)
+        for t in range(RUN):
+            quantise_x(0, t)
+        warm_up(0, WARM_FIRST)
+        copy_g(V, 0, 0, 2)
+        copy_g(S, 0, 2, 2)
+        quantise_x(1, 0)
+        warm_up(2, WARM_SECOND)
+        copy_g(V, 1, 0, 2)
+        copy_g(S, 1, 2, 2)
+        quantise_x(1, 1)
+        copy_g(V, 2, 0, 2)
+        copy_g(S, 2, 2, 1)
+        quantise_x(1, 2)
+        copy_g(V, 3, 0, 1)
+        copy_g(S, 3, 1, 1)
+        for t in range(RUN):
+            quantise_g(t, 1)
+        passes(0)
+        quantise_g(RUN, 2)
+        quantise_g(RUN + 2, 2)
+        passes(1)
+        quantise_x(1, 3)
+        copy_g(S, 3, 2, 1)
+        quantise_g(2 * RUN, RUN)
+        passes(2)
+        copy_g(S, 2, 3, 1)
+        copy_g(V, 3, 3, 1)
+        quantise_g(3 * RUN, RUN)
+        passes(3)
+        empty(S, 0)
+        empty(S, 1)
+        empty(V, 2)
+        empty(S, 3)
         nc.sync.dma_start(out=out.rearrange("f c h w -> f (c h w)"), in_=result[:].rearrange("p c a -> p (c a)"))

@@ -17,15 +17,15 @@ FREQS = 16
 RUN = 4
 GROUPS = FREQS // RUN
 N_MOVING = 512
-X_CHUNKS = (16, 16, 32)
-G_CHUNKS = (32, 32, 32, 32)
+HALF_PACK = 2
+G_CHUNKS = (48, 48, 32)
 TWINS = 2
 UNIT = TWINS * CHANNELS
 SEQ_UNITS = 11
 UNIT_PLACE = (0, 6, 9, 4)
 ZERO_RUNS = ((1, 3), (5, 1), (7, 2), (10, 1))
-WARM_FIRST = 5
-WARM_SECOND = 3
+WARM_FIRST = 4
+WARM_LATER = 2
 
 FLOPS = 2 * FREQS * FILTERS * CHANNELS * IMAGES
 BYTES = 2 * IMAGES * FREQS * (CHANNELS + FILTERS) + 4 * FILTERS * CHANNELS * FREQS
@@ -38,14 +38,10 @@ def tile_convdct_pa_s_kernel(tc, x_dct, k_dct, grad_out, out):
 
     with tc.tile_pool(name="keep", bufs=1) as keep, tc.psum_pool(name="psum", bufs=1) as psum, tc.manual_schedule():
         x_raw = []
-        x_first = []
-        first = 0
-        for c, rows in enumerate(X_CHUNKS):
-            chunk = keep.tile([P, PACK, rows * FREQS], BF16, name="x_raw%d" % c)
-            nc.sync.dma_start(out=chunk[:], in_=x_rows[:, :, first * FREQS : (first + rows) * FREQS])
+        for u in range(PACK // HALF_PACK):
+            chunk = keep.tile([P, HALF_PACK, CHANNELS * FREQS], BF16, name="x_raw%d" % u)
+            nc.sync.dma_start(out=chunk[:], in_=x_rows[:, u * HALF_PACK : (u + 1) * HALF_PACK, :])
             x_raw.append(chunk)
-            x_first.append(first)
-            first += rows
         g_raw = []
         g_first = []
         first = 0
@@ -77,10 +73,10 @@ def tile_convdct_pa_s_kernel(tc, x_dct, k_dct, grad_out, out):
         result = keep.tile([P, CHANNELS, FREQS], F32)
         banks = {}
 
-        def copy_x(copy, c, m):
-            rows = slice(x_first[c], x_first[c] + X_CHUNKS[c])
-            src = x_raw[c][:].rearrange("p j (r m s t) -> p m s r j t", m=TWINS, s=TWINS, t=RUN)
-            dst = x_grouped[:, :, :, :, rows, :].rearrange("p m t s r j -> p m s r j t")
+        def copy_x(copy, u, m):
+            images = slice(u * HALF_PACK, (u + 1) * HALF_PACK)
+            src = x_raw[u][:].rearrange("p j (r m s t) -> p m s r j t", m=TWINS, s=TWINS, t=RUN)
+            dst = x_grouped[:, :, :, :, :, images].rearrange("p m t s r j -> p m s r j t")
             copy(out=dst[:, m], in_=src[:, m])
 
         def copy_g(copy, c, first_group, count):
@@ -113,14 +109,14 @@ def tile_convdct_pa_s_kernel(tc, x_dct, k_dct, grad_out, out):
 
         warm = psum.tile([P, N_MOVING], F32, name="warm")
 
-        def warm_up(group, count):
+        def warm_up(group, t, count):
             for i in range(count):
                 nc.tensor.matmul_mx(
                     out=warm[:],
                     lhsT=zero_codes[:].bitcast(E5M2_X4),
                     lhsT_scale=zero_scales[:],
-                    rhs=x_codes[:, window(group, 0)].bitcast(E4M3_X4),
-                    rhs_scale=x_scales[:, window(group, 0)],
+                    rhs=x_codes[:, window(group, t)].bitcast(E4M3_X4),
+                    rhs_scale=x_scales[:, window(group, t)],
                     start=True,
                     stop=True,
                 )
@@ -150,24 +146,21 @@ def tile_convdct_pa_s_kernel(tc, x_dct, k_dct, grad_out, out):
         copy_x(V, 0, 0)
         copy_x(S, 0, 1)
         copy_x(V, 1, 0)
-        copy_x(V, 1, 1)
-        copy_x(V, 2, 0)
-        copy_x(S, 2, 1)
+        copy_x(S, 1, 1)
         for t in range(RUN):
             quantise_x(0, t)
-        warm_up(0, WARM_FIRST)
+        warm_up(0, 0, WARM_FIRST)
         copy_g(V, 0, 0, 2)
         copy_g(S, 0, 2, 2)
         quantise_x(1, 0)
-        warm_up(2, WARM_SECOND)
+        warm_up(2, 0, WARM_LATER)
         copy_g(V, 1, 0, 2)
-        copy_g(S, 1, 2, 2)
+        copy_g(S, 1, 2, 1)
         quantise_x(1, 1)
-        copy_g(V, 2, 0, 2)
-        copy_g(S, 2, 2, 1)
+        warm_up(2, 1, WARM_LATER)
+        copy_g(V, 2, 0, 1)
+        copy_g(S, 2, 1, 1)
         quantise_x(1, 2)
-        copy_g(V, 3, 0, 1)
-        copy_g(S, 3, 1, 1)
         for t in range(RUN):
             quantise_g(t, 1)
         passes(0)
@@ -175,15 +168,16 @@ def tile_convdct_pa_s_kernel(tc, x_dct, k_dct, grad_out, out):
         quantise_g(RUN + 2, 2)
         passes(1)
         quantise_x(1, 3)
-        copy_g(S, 3, 2, 1)
+        copy_g(S, 2, 2, 1)
         quantise_g(2 * RUN, RUN)
         passes(2)
+        copy_g(S, 1, 3, 1)
         copy_g(S, 2, 3, 1)
-        copy_g(V, 3, 3, 1)
-        quantise_g(3 * RUN, RUN)
+        quantise_g(3 * RUN, 2)
+        quantise_g(3 * RUN + 2, 2)
         passes(3)
         empty(S, 0)
         empty(S, 1)
-        empty(V, 2)
-        empty(S, 3)
+        empty(S, 2)
+        empty(V, 3)
         nc.sync.dma_start(out=out.rearrange("f c h w -> f (c h w)"), in_=result[:].rearrange("p c a -> p (c a)"))

@@ -56,10 +56,12 @@ def tile_convdct_pa_s_kernel(tc, x_dct, k_dct, grad_out, out):
         x_width = TWINS * half + CHANNELS
         x_codes = keep.tile([P, x_width], U32, align_bytes=64)
         x_scales = keep.tile([P, x_width], U8, align_bytes=64)
-        nc.gpsimd.memset(x_scales[:].bitcast(F32), 0.0)
-        nc.gpsimd.memset(x_codes[:, half:].bitcast(F32), 0.0)
+        for start, count in ZERO_RUNS:
+            nc.gpsimd.memset(x_codes[:, half + start * UNIT : half + (start + count) * UNIT].bitcast(F32), 0.0)
+        nc.gpsimd.memset(x_codes[:, TWINS * half :].bitcast(F32), 0.0)
         for start, count in ZERO_RUNS:
             nc.vector.memset(x_codes[:, start * UNIT : (start + count) * UNIT].bitcast(I32), 0)
+        nc.vector.memset(x_scales[:].bitcast(I32), 0)
         zeros = keep.tile([P, FILTERS * PACK], BF16, align_bytes=64)
         zero_codes = keep.tile([P, FILTERS], U32, align_bytes=64)
         zero_scales = keep.tile([P, FILTERS], U8, align_bytes=64)

@@ -143,6 +143,18 @@ def tile_convdct_pa_s_kernel(tc, x_dct, k_dct, grad_out, out):
             wanted = banks[group][:].rearrange("p (t e c) -> p e c t", t=RUN, e=TWINS)
             copy(out=result[:, :, group * RUN : (group + 1) * RUN], in_=wanted[:, 0])
 
+        def empty_half(copy, group, h):
+            channels = slice(h * CHANNELS // 2, (h + 1) * CHANNELS // 2)
+            wanted = banks[group][:].rearrange("p (t e c) -> p e c t", t=RUN, e=TWINS)
+            copy(out=result[:, channels, group * RUN : (group + 1) * RUN], in_=wanted[:, 0, channels])
+
+        def store_half(queue, h):
+            channels = slice(h * CHANNELS // 2, (h + 1) * CHANNELS // 2)
+            queue.dma_start(
+                out=out.rearrange("f c h w -> f c (h w)")[:, channels],
+                in_=result[:, channels],
+            )
+
         V = nc.vector.tensor_copy
         S = nc.scalar.copy
         copy_x(V, 0, 0)
@@ -181,5 +193,7 @@ def tile_convdct_pa_s_kernel(tc, x_dct, k_dct, grad_out, out):
         empty(S, 0)
         empty(S, 1)
         empty(S, 2)
-        empty(V, 3)
-        nc.sync.dma_start(out=out.rearrange("f c h w -> f (c h w)"), in_=result[:].rearrange("p c a -> p (c a)"))
+        empty_half(V, 3, 0)
+        store_half(nc.sync, 0)
+        empty_half(V, 3, 1)
+        store_half(nc.scalar, 1)

@@ -18,12 +18,12 @@ RUN = 4
 GROUPS = FREQS // RUN
 N_MOVING = 512
 HALF_PACK = 2
-G_CHUNKS = (48, 48, 32)
+G_CHUNKS = (64, 48, 16)
 TWINS = 2
 UNIT = TWINS * CHANNELS
-SEQ_UNITS = 11
-UNIT_PLACE = (0, 6, 9, 4)
-ZERO_RUNS = ((1, 3), (5, 1), (7, 2), (10, 1))
+SEQ_UNITS = 12
+UNIT_PLACE = (0, 7, 10, 5)
+ZERO_RUNS = ((1, 4), (6, 1), (8, 2), (11, 1))
 WARM_FIRST = 4
 WARM_LATER = 2
 
@@ -53,12 +53,11 @@ def tile_convdct_pa_s_kernel(tc, x_dct, k_dct, grad_out, out):
             first += rows
 
         half = SEQ_UNITS * UNIT
-        x_width = TWINS * half + CHANNELS
-        x_codes = keep.tile([P, x_width], U32, align_bytes=64)
-        x_scales = keep.tile([P, x_width], U8, align_bytes=64)
+        x_width = TWINS * half
+        x_codes = keep.tile([P, x_width], U32, align_bytes=256)
+        x_scales = keep.tile([P, x_width], U8, align_bytes=256)
         for start, count in ZERO_RUNS:
             nc.gpsimd.memset(x_codes[:, half + start * UNIT : half + (start + count) * UNIT].bitcast(F32), 0.0)
-        nc.gpsimd.memset(x_codes[:, TWINS * half :].bitcast(F32), 0.0)
         for start, count in ZERO_RUNS:
             nc.vector.memset(x_codes[:, start * UNIT : (start + count) * UNIT].bitcast(I32), 0)
         nc.vector.memset(x_scales[:].bitcast(I32), 0)
@@ -70,8 +69,8 @@ def tile_convdct_pa_s_kernel(tc, x_dct, k_dct, grad_out, out):
 
         x_grouped = keep.tile([P, TWINS, RUN, TWINS, CHANNELS, PACK], BF16, align_bytes=64)
         g_grouped = keep.tile([P, FREQS, FILTERS, PACK], BF16, align_bytes=64)
-        g_codes = keep.tile([P, FREQS * FILTERS], U32, align_bytes=64)
-        g_scales = keep.tile([P, FREQS * FILTERS], U8, align_bytes=64)
+        g_codes = keep.tile([P, FREQS * FILTERS], U32, align_bytes=256)
+        g_scales = keep.tile([P, FREQS * FILTERS], U8, align_bytes=256)
         result = keep.tile([P, CHANNELS, FREQS], F32)
         banks = {}
 
@@ -104,9 +103,7 @@ def tile_convdct_pa_s_kernel(tc, x_dct, k_dct, grad_out, out):
             )
 
         def window(group, t):
-            m = group // TWINS
-            s = group % TWINS
-            start = (m * SEQ_UNITS + UNIT_PLACE[t] - t) * UNIT + s * CHANNELS
+            start = (group // TWINS * SEQ_UNITS + UNIT_PLACE[t] - t) * UNIT
             return slice(start, start + N_MOVING)
 
         warm = psum.tile([P, N_MOVING], F32, name="warm")
@@ -141,12 +138,12 @@ def tile_convdct_pa_s_kernel(tc, x_dct, k_dct, grad_out, out):
 
         def empty(copy, group):
             wanted = banks[group][:].rearrange("p (t e c) -> p e c t", t=RUN, e=TWINS)
-            copy(out=result[:, :, group * RUN : (group + 1) * RUN], in_=wanted[:, 0])
+            copy(out=result[:, :, group * RUN : (group + 1) * RUN], in_=wanted[:, group % TWINS])
 
         def empty_half(copy, group, h):
             channels = slice(h * CHANNELS // 2, (h + 1) * CHANNELS // 2)
             wanted = banks[group][:].rearrange("p (t e c) -> p e c t", t=RUN, e=TWINS)
-            copy(out=result[:, channels, group * RUN : (group + 1) * RUN], in_=wanted[:, 0, channels])
+            copy(out=result[:, channels, group * RUN : (group + 1) * RUN], in_=wanted[:, group % TWINS, channels])
 
         def store_half(queue, h):
             channels = slice(h * CHANNELS // 2, (h + 1) * CHANNELS // 2)
@@ -164,26 +161,26 @@ def tile_convdct_pa_s_kernel(tc, x_dct, k_dct, grad_out, out):
         for t in range(RUN):
             quantise_x(0, t)
         warm_up(0, 0, WARM_FIRST)
-        copy_g(V, 0, 0, 2)
-        copy_g(S, 0, 2, 2)
-        quantise_x(1, 0)
-        warm_up(2, 0, WARM_LATER)
-        copy_g(V, 1, 0, 2)
-        copy_g(S, 1, 2, 1)
-        quantise_x(1, 1)
-        warm_up(2, 1, WARM_LATER)
+        warm_up(0, 1, WARM_LATER)
+        warm_up(0, 2, WARM_LATER)
+        copy_g(V, 0, 0, 3)
+        copy_g(S, 0, 3, 1)
+        copy_g(V, 1, 0, 1)
+        copy_g(S, 1, 1, 1)
         copy_g(V, 2, 0, 1)
         copy_g(S, 2, 1, 1)
-        quantise_x(1, 2)
         for t in range(RUN):
             quantise_g(t, 1)
         passes(0)
         quantise_g(RUN, 2)
         quantise_g(RUN + 2, 2)
         passes(1)
-        quantise_x(1, 3)
+        for t in range(RUN):
+            quantise_x(1, t)
+        copy_g(S, 1, 2, 1)
         copy_g(S, 2, 2, 1)
-        quantise_g(2 * RUN, RUN)
+        quantise_g(2 * RUN, 2)
+        quantise_g(2 * RUN + 2, 2)
         passes(2)
         copy_g(S, 1, 3, 1)
         copy_g(S, 2, 3, 1)

@@ -17,7 +17,6 @@ FREQS = 16
 RUN = 4
 GROUPS = FREQS // RUN
 N_MOVING = 512
-HALF_PACK = 2
 G_CHUNKS = (64, 48, 16)
 TWINS = 2
 UNIT = TWINS * CHANNELS
@@ -37,11 +36,8 @@ def tile_convdct_pa_s_kernel(tc, x_dct, k_dct, grad_out, out):
     g_rows = grad_out.rearrange("(p j) f h w -> p j (f h w)", j=PACK)
 
     with tc.tile_pool(name="keep", bufs=1) as keep, tc.psum_pool(name="psum", bufs=1) as psum, tc.manual_schedule():
-        x_raw = []
-        for u in range(PACK // HALF_PACK):
-            chunk = keep.tile([P, HALF_PACK, CHANNELS * FREQS], BF16, name="x_raw%d" % u)
-            nc.sync.dma_start(out=chunk[:], in_=x_rows[:, u * HALF_PACK : (u + 1) * HALF_PACK, :])
-            x_raw.append(chunk)
+        x_raw = keep.tile([P, PACK, CHANNELS * FREQS], BF16)
+        nc.sync.dma_start(out=x_raw[:], in_=x_rows)
         g_raw = []
         g_first = []
         first = 0
@@ -74,10 +70,9 @@ def tile_convdct_pa_s_kernel(tc, x_dct, k_dct, grad_out, out):
         result = keep.tile([P, CHANNELS, FREQS], F32)
         banks = {}
 
-        def copy_x(copy, u, m):
-            images = slice(u * HALF_PACK, (u + 1) * HALF_PACK)
-            src = x_raw[u][:].rearrange("p j (r m s t) -> p m s r j t", m=TWINS, s=TWINS, t=RUN)
-            dst = x_grouped[:, :, :, :, :, images].rearrange("p m t s r j -> p m s r j t")
+        def copy_x(copy, m):
+            src = x_raw[:].rearrange("p j (r m s t) -> p m s r j t", m=TWINS, s=TWINS, t=RUN)
+            dst = x_grouped[:].rearrange("p m t s r j -> p m s r j t")
             copy(out=dst[:, m], in_=src[:, m])
 
         def copy_g(copy, c, first_group, count):
@@ -154,10 +149,8 @@ def tile_convdct_pa_s_kernel(tc, x_dct, k_dct, grad_out, out):
 
         V = nc.vector.tensor_copy
         S = nc.scalar.copy
-        copy_x(V, 0, 0)
-        copy_x(S, 0, 1)
-        copy_x(V, 1, 0)
-        copy_x(S, 1, 1)
+        copy_x(V, 0)
+        copy_x(S, 1)
         for t in range(RUN):
             quantise_x(0, t)
         warm_up(0, 0, WARM_FIRST)
@@ -193,4 +186,4 @@ def tile_convdct_pa_s_kernel(tc, x_dct, k_dct, grad_out, out):
         empty_half(V, 3, 0)
         store_half(nc.sync, 0)
         empty_half(V, 3, 1)
-        store_half(nc.scalar, 1)
+        store_half(nc.sync, 1)

@@ -176,7 +176,7 @@ def tile_convdct_pa_s_kernel(tc, x_dct, k_dct, grad_out, out):
         quantise_g(2 * RUN + 2, 2)
         passes(2)
         copy_g(S, 1, 3, 1)
-        copy_g(S, 2, 3, 1)
+        copy_g(V, 2, 3, 1)
         quantise_g(3 * RUN, 2)
         quantise_g(3 * RUN + 2, 2)
         passes(3)

import concourse.mybir as mybir

BF16 = mybir.dt.bfloat16
F32 = mybir.dt.float32
U32 = mybir.dt.uint32
U8 = mybir.dt.uint8
I32 = mybir.dt.int32
E4M3_X4 = mybir.dt.float8_e4m3fn_x4
E5M2_X4 = mybir.dt.float8_e5m2_x4

P = 128
PACK = 4
IMAGES = P * PACK
CHANNELS = 64
FILTERS = 128
FREQS = 16
RUN = 4
GROUPS = FREQS // RUN
N_MOVING = 512
G_CHUNKS = (64, 48, 16)
TWINS = 2
UNIT = TWINS * CHANNELS
SEQ_UNITS = 12
UNIT_PLACE = (0, 7, 10, 5)
ZERO_RUNS = ((1, 4), (6, 1), (8, 2), (11, 1))
WARM_FIRST = 4
WARM_LATER = 2

FLOPS = 2 * FREQS * FILTERS * CHANNELS * IMAGES
BYTES = 2 * IMAGES * FREQS * (CHANNELS + FILTERS) + 4 * FILTERS * CHANNELS * FREQS


def tile_convdct_pa_s_kernel(tc, x_dct, k_dct, grad_out, out):
    nc = tc.nc
    x_rows = x_dct.rearrange("(p j) c h w -> p j (c h w)", j=PACK)
    g_rows = grad_out.rearrange("(p j) f h w -> p j (f h w)", j=PACK)

    with tc.tile_pool(name="keep", bufs=1) as keep, tc.psum_pool(name="psum", bufs=1) as psum, tc.manual_schedule():
        x_raw = keep.tile([P, PACK, CHANNELS * FREQS], BF16)
        nc.sync.dma_start(out=x_raw[:], in_=x_rows)
        g_raw = []
        g_first = []
        first = 0
        for c, rows in enumerate(G_CHUNKS):
            chunk = keep.tile([P, PACK, rows * FREQS], BF16, name="g_raw%d" % c)
            nc.sync.dma_start(out=chunk[:], in_=g_rows[:, :, first * FREQS : (first + rows) * FREQS])
            g_raw.append(chunk)
            g_first.append(first)
            first += rows

        half = SEQ_UNITS * UNIT
        x_width = TWINS * half
        x_codes = keep.tile([P, x_width], U32, align_bytes=256)
        x_scales = keep.tile([P, x_width], U8, align_bytes=256)
        for start, count in ZERO_RUNS:
            nc.gpsimd.memset(x_codes[:, half + start * UNIT : half + (start + count) * UNIT].bitcast(F32), 0.0)
        for start, count in ZERO_RUNS:
            nc.vector.memset(x_codes[:, start * UNIT : (start + count) * UNIT].bitcast(I32), 0)
        nc.vector.memset(x_scales[:].bitcast(I32), 0)
        zeros = keep.tile([P, FILTERS * PACK], BF16, align_bytes=64)
        zero_codes = keep.tile([P, FILTERS], U32, align_bytes=64)
        zero_scales = keep.tile([P, FILTERS], U8, align_bytes=64)
        nc.vector.memset(zeros[:].bitcast(I32), 0)
        nc.vector.quantize_mx(out=zero_codes[:].bitcast(E5M2_X4), scales=zero_scales[:], in_=zeros[:])

        x_grouped = keep.tile([P, TWINS, RUN, TWINS, CHANNELS, PACK], BF16, align_bytes=64)
        g_grouped = keep.tile([P, FREQS, FILTERS, PACK], BF16, align_bytes=64)
        g_codes = keep.tile([P, FREQS * FILTERS], U32, align_bytes=256)
        g_scales = keep.tile([P, FREQS * FILTERS], U8, align_bytes=256)
        result = keep.tile([P, CHANNELS, FREQS], F32)
        banks = {}

        def copy_x(copy, m):
            src = x_raw[:].rearrange("p j (r m s t) -> p m s r j t", m=TWINS, s=TWINS, t=RUN)
            dst = x_grouped[:].rearrange("p m t s r j -> p m s r j t")
            copy(out=dst[:, m], in_=src[:, m])

        def copy_g(copy, c, first_group, count):
            rows = slice(g_first[c], g_first[c] + G_CHUNKS[c])
            src = g_raw[c][:].rearrange("p j (r a t) -> p a r j t", a=GROUPS, t=RUN)
            dst = g_grouped[:, :, rows, :].rearrange("p (a t) r j -> p a r j t", t=RUN)
            copy(out=dst[:, first_group : first_group + count], in_=src[:, first_group : first_group + count])

        def quantise_x(m, t):
            start = (m * SEQ_UNITS + UNIT_PLACE[t]) * UNIT
            nc.vector.quantize_mx(
                out=x_codes[:, start : start + UNIT].bitcast(E4M3_X4),
                scales=x_scales[:, start : start + UNIT],
                in_=x_grouped[:, m, t].rearrange("p s r j -> p (s r j)"),
            )

        def quantise_g(first_freq, count):
            columns = slice(first_freq * FILTERS, (first_freq + count) * FILTERS)
            nc.vector.quantize_mx(
                out=g_codes[:, columns].bitcast(E5M2_X4),
                scales=g_scales[:, columns],
                in_=g_grouped[:, first_freq : first_freq + count].rearrange("p a f j -> p (a f j)"),
            )

        def window(group, t):
            start = (group // TWINS * SEQ_UNITS + UNIT_PLACE[t] - t) * UNIT
            return slice(start, start + N_MOVING)

        warm = psum.tile([P, N_MOVING], F32, name="warm")

        def warm_up(group, t, count):
            for i in range(count):
                nc.tensor.matmul_mx(
                    out=warm[:],
                    lhsT=zero_codes[:].bitcast(E5M2_X4),
                    lhsT_scale=zero_scales[:],
                    rhs=x_codes[:, window(group, t)].bitcast(E4M3_X4),
                    rhs_scale=x_scales[:, window(group, t)],
                    start=True,
                    stop=True,
                )

        def passes(group):
            bank = psum.tile([P, N_MOVING], F32, name="bank%d" % group)
            banks[group] = bank
            for t in range(RUN):
                freq = group * RUN + t
                columns = slice(freq * FILTERS, (freq + 1) * FILTERS)
                nc.tensor.matmul_mx(
                    out=bank[:],
                    lhsT=g_codes[:, columns].bitcast(E5M2_X4),
                    lhsT_scale=g_scales[:, columns],
                    rhs=x_codes[:, window(group, t)].bitcast(E4M3_X4),
                    rhs_scale=x_scales[:, window(group, t)],
                    start=(t == 0),
                    stop=(t == RUN - 1),
                )

        def empty(copy, group):
            wanted = banks[group][:].rearrange("p (t e c) -> p e c t", t=RUN, e=TWINS)
            copy(out=result[:, :, group * RUN : (group + 1) * RUN], in_=wanted[:, group % TWINS])

        def empty_half(copy, group, h):
            channels = slice(h * CHANNELS // 2, (h + 1) * CHANNELS // 2)
            wanted = banks[group][:].rearrange("p (t e c) -> p e c t", t=RUN, e=TWINS)
            copy(out=result[:, channels, group * RUN : (group + 1) * RUN], in_=wanted[:, group % TWINS, channels])

        def store_half(queue, h):
            channels = slice(h * CHANNELS // 2, (h + 1) * CHANNELS // 2)
            queue.dma_start(
                out=out.rearrange("f c h w -> f c (h w)")[:, channels],
                in_=result[:, channels],
            )

        V = nc.vector.tensor_copy
        S = nc.scalar.copy
        copy_x(V, 0)
        copy_x(S, 1)
        for t in range(RUN):
            quantise_x(0, t)
        warm_up(0, 0, WARM_FIRST)
        warm_up(0, 1, WARM_LATER)
        warm_up(0, 2, WARM_LATER)
        copy_g(V, 0, 0, 3)
        copy_g(S, 0, 3, 1)
        copy_g(V, 1, 0, 1)
        copy_g(S, 1, 1, 1)
        copy_g(V, 2, 0, 1)
        copy_g(S, 2, 1, 1)
        for t in range(RUN):
            quantise_g(t, 1)
        passes(0)
        quantise_g(RUN, 2)
        quantise_g(RUN + 2, 2)
        passes(1)
        for t in range(RUN):
            quantise_x(1, t)
        copy_g(S, 1, 2, 1)
        copy_g(S, 2, 2, 1)
        quantise_g(2 * RUN, 2)
        quantise_g(2 * RUN + 2, 2)
        passes(2)
        copy_g(S, 1, 3, 1)
        copy_g(V, 2, 3, 1)
        quantise_g(3 * RUN, 2)
        quantise_g(3 * RUN + 2, 2)
        passes(3)
        empty(S, 0)
        empty(S, 1)
        empty(S, 2)
        empty_half(V, 3, 0)
        store_half(nc.sync, 0)
        empty_half(V, 3, 1)
        store_half(nc.sync, 1)
